import numpy as np
import ml_dtypes


def mxq(x, axis, fmt="e4m3"):
    dtype, down = {"e4m3": (ml_dtypes.float8_e4m3fn, 7), "e5m2": (ml_dtypes.float8_e5m2, 14)}[fmt]
    v = np.moveaxis(np.asarray(x, np.float32).astype(ml_dtypes.bfloat16).astype(np.float64), axis, -1)
    blocks = v.reshape(v.shape[:-1] + (-1, 32))
    amax = np.abs(blocks).max(-1, keepdims=True)
    byte = np.maximum(np.where(amax > 0, np.frexp(amax)[1] - 1 + 127, 0) - down, 1)
    scale = np.exp2(byte - 127.0)
    codes = (blocks / scale).astype(np.float32).astype(dtype).astype(np.float64)
    return np.moveaxis((codes * scale).reshape(v.shape), -1, axis)


WIDE = False


def mx_kscale(k):
    if not WIDE:
        return np.ones(k)
    levels = np.array([10, -10, 5, -5, 0])
    a = np.random.permutation(np.resize(levels, k // 512 * 4)).reshape(k // 512, 4)
    idx = np.arange(k)
    return np.exp2(a[idx // 512, idx % 128 // 32])


BF16 = ml_dtypes.bfloat16


def bf(x):
    return np.asarray(x, np.float32).astype(BF16)


def f64(x):
    return np.asarray(x).astype(np.float64)


B, N, DIM, H, DK, DV, KB = 8, 1024, 512, 2, 16, 48, 512
WT = 256.0
EPS = 1e-12
DI = H * (DK + DV)


def l2norm(t):
    n = np.sqrt((t * t).sum(-1, keepdims=True))
    return t / np.maximum(n, EPS)


def setup_inputs():
    s = mx_kscale(DIM)
    return {'tokens': bf(np.random.standard_normal((B, N, DIM)) * s),
            'w_qg': bf(np.random.standard_normal((DI, DIM)) / np.sqrt(DIM) / s[None, :]),
            'w_kv': bf(np.random.standard_normal((DI, DIM)) / np.sqrt(DIM) / s[None, :]),
            'sm_log': bf(np.linspace(3.0, 5.8, H) + 0.1 * np.random.standard_normal(H))}


def reference(tokens, w_qg, w_kv, sm_log):
    tq = mxq(f64(tokens), 2, 'e4m3')
    qg = (tq @ mxq(f64(w_qg), 1, 'e4m3').T).reshape(B, N, H, DK + DV).transpose(0, 2, 1, 3)
    kv = (tq @ mxq(f64(w_kv), 1, 'e4m3').T).reshape(B, N, H, DK + DV).transpose(0, 2, 1, 3)
    q, g = qg[..., :DK], qg[..., DK:]
    k, v = kv[..., :DK], kv[..., DK:]
    q, k, v = l2norm(q), l2norm(k), l2norm(v)
    w = np.exp(f64(sm_log)) + 1.0
    gamma = np.where(w < WT, 0.5 * (np.cos(np.pi * w / WT) + 1.0), 0.0)
    freq = np.pi * gamma / w
    ang = freq[:, None] * np.arange(N, dtype=np.float64)[None, :]
    cos = np.cos(ang)[None, :, :, None]
    sin = np.sin(ang)[None, :, :, None]

    def rotate(t):
        x0, x1 = t[..., 0:1], t[..., 1:2]
        return np.concatenate([x0 * cos - x1 * sin, x0 * sin + x1 * cos, t[..., 2:]], axis=-1)

    gate = np.tanh(g / (1.0 + np.exp(-g)))
    return rotate(q), gate, rotate(k), v

@@ -1,0 +1,276 @@
+import math
+from contextlib import ExitStack
+
+import concourse.mybir as mybir
+from concourse.masks import make_identity
+
+F32 = mybir.dt.float32
+BF16 = mybir.dt.bfloat16
+I32 = mybir.dt.int32
+U32 = mybir.dt.uint32
+U8 = mybir.dt.uint8
+FP8X4 = mybir.dt.float8_e4m3fn_x4
+ACT = mybir.ActivationFunctionType
+ALU = mybir.AluOpType
+AXIS = mybir.AxisListType
+
+B, N, DIM, H, DK, DV = 8, 1024, 512, 2, 16, 48
+HEAD = DK + DV
+COLS = 2 * H * HEAD
+CHUNKS = 2 * H
+WT = 256.0
+EPS = 1e-12
+
+P = 128
+PACK = 4
+T = N // P
+PAIRS = T // 2
+WORDS = DIM // 2
+NARROW = T * CHUNKS
+WIDE = T * H
+
+ROUND_MAGIC = 1.5 * 2.0**23
+LOG_MAX = 6.0
+
+FLOPS = 2 * B * N * DIM * COLS
+
+
+def tile_gatedscreeningtile_pa_t_kernel(
+    tc, tokens, w_qg, w_kv, sm_log, out_0, out_1, out_2, out_3
+):
+    nc = tc.nc
+    with ExitStack() as ctx:
+        const = ctx.enter_context(tc.tile_pool(name="const", bufs=1))
+        resident = ctx.enter_context(tc.tile_pool(name="resident", bufs=1))
+        stage = ctx.enter_context(tc.tile_pool(name="stage", bufs=4))
+        work = ctx.enter_context(tc.tile_pool(name="work", bufs=2))
+        results = ctx.enter_context(tc.tile_pool(name="results", bufs=3))
+
+        w_rows = const.tile([P, 2, DIM], BF16)
+        nc.sync.dma_start(out=w_rows[:, 0, :], in_=w_qg)
+        nc.sync.dma_start(out=w_rows[:, 1, :], in_=w_kv)
+        x_rows = []
+        for b in range(B):
+            x_b = resident.tile([P, T, DIM], BF16, name="x_rows%d" % b)
+            nc.sync.dma_start(out=x_b[:], in_=tokens[b].rearrange("(p t) k -> p t k", t=T))
+            x_rows.append(x_b)
+        log_window = const.tile([P, H], BF16)
+        nc.sync.dma_start(out=log_window[:], in_=sm_log.partition_broadcast(P))
+
+        warm = const.tile([P, 1], F32)
+        nc.vector.memset(warm[:], 0.0)
+        nc.scalar.activation(out=warm[:], in_=warm[:], func=ACT.Silu)
+
+        ident = const.tile([P, P], F32)
+        make_identity(nc, ident[:])
+
+        def flip(rows, first):
+            words = rows[:].bitcast(F32)
+            flipped = flip_banks.tile([P, 2, 2, P], F32, tag="flipped")
+            for j in range(2):
+                for u in range(2):
+                    nc.tensor.transpose(
+                        flipped[:, j, u, :], words[:, first + j, u * P : (u + 1) * P], ident[:]
+                    )
+            return flipped
+
+        def quantise(flipped, copy, codes, scales):
+            grouped = stage.tile([P, 2 * P * PACK], BF16, tag="grouped", align_bytes=64)
+            copy(
+                out=grouped[:].bitcast(F32).rearrange("p (j r u) -> p j r u", j=2, u=2),
+                in_=flipped[:].rearrange("p j u r -> p j r u"),
+            )
+            nc.vector.quantize_mx(out=codes.bitcast(FP8X4), scales=scales, in_=grouped[:])
+
+        w_codes = const.tile([P, COLS], U32, align_bytes=64)
+        w_scales = const.tile([P, COLS], U8, align_bytes=64)
+
+        x_codes = []
+        x_scales = []
+        for b in range(B):
+            x_codes.append(resident.tile([P, T * P], U32, name="x_codes%d" % b, align_bytes=64))
+            x_scales.append(resident.tile([P, T * P], U8, name="x_scales%d" % b, align_bytes=64))
+
+        def quantise_batch(b):
+            flipped = [flip(x_rows[b], 2 * i) for i in range(PAIRS)]
+            for i in range(PAIRS):
+                copy = nc.scalar.copy if i % 2 == 0 else nc.vector.tensor_copy
+                cols = slice(2 * i * P, (2 * i + 2) * P)
+                quantise(flipped[i], copy, x_codes[b][:, cols], x_scales[b][:, cols])
+
+        def project(banks, b, i):
+            acc = banks.tile([P, 2, COLS], F32, tag="acc")
+            for j in range(2):
+                cols = slice((2 * i + j) * P, (2 * i + j + 1) * P)
+                nc.tensor.matmul_mx(
+                    out=acc[:, j, :],
+                    lhsT=x_codes[b][:, cols].bitcast(FP8X4),
+                    lhsT_scale=x_scales[b][:, cols],
+                    rhs=w_codes[:].bitcast(FP8X4),
+                    rhs_scale=w_scales[:],
+                    start=True,
+                    stop=True,
+                )
+            return acc[:].rearrange("p j (c d) -> p j c d", d=HEAD)
+
+        window = const.tile([P, H], F32)
+        two = const.tile([P, H], F32)
+        nc.gpsimd.memset(two[:], 2.0)
+        nc.gpsimd.tensor_scalar(
+            out=window[:], in0=log_window[:], scalar1=LOG_MAX, scalar2=1.0 / math.log(2.0),
+            op0=ALU.min, op1=ALU.mult,
+        )
+        nc.gpsimd.tensor_tensor(out=window[:], in0=two[:], in1=window[:], op=ALU.pow)
+        nc.gpsimd.tensor_scalar(
+            out=window[:], in0=window[:], scalar1=1.0, scalar2=WT, op0=ALU.add, op1=ALU.min
+        )
+        cos_window = const.tile([P, H], F32)
+        nc.scalar.activation(
+            out=cos_window[:], in_=window[:], func=ACT.Sin, scale=-math.pi / WT, bias=math.pi / 2
+        )
+        per_position = const.tile([P, H], F32)
+        nc.vector.reciprocal(out=per_position[:], in_=window[:])
+        nc.vector.scalar_tensor_tensor(
+            out=per_position[:], in0=cos_window[:], scalar=1.0, in1=per_position[:],
+            op0=ALU.add, op1=ALU.mult,
+        )
+        position_int = const.tile([P, T], I32)
+        nc.gpsimd.iota(position_int[:], pattern=[[1, T]], base=0, channel_multiplier=T)
+        position = const.tile([P, T], F32)
+        nc.vector.tensor_copy(out=position[:], in_=position_int[:])
+        turns = const.tile([P, H, T], F32)
+        for h in range(H):
+            nc.vector.tensor_scalar(
+                out=turns[:, h, :], in0=position[:], scalar1=per_position[:, h : h + 1],
+                scalar2=0.25, op0=ALU.mult, op1=ALU.mult,
+            )
+        whole = const.tile([P, H, T], F32)
+        nc.vector.tensor_scalar(
+            out=whole[:], in0=turns[:], scalar1=ROUND_MAGIC, scalar2=ROUND_MAGIC,
+            op0=ALU.add, op1=ALU.subtract,
+        )
+        nc.vector.tensor_sub(out=turns[:], in0=turns[:], in1=whole[:])
+        sin_half = const.tile([P, H, T], F32)
+        sin_quarter = const.tile([P, H, T], F32)
+        nc.scalar.activation(out=sin_half[:], in_=turns[:], func=ACT.Sin, scale=math.pi)
+        nc.scalar.activation(out=sin_quarter[:], in_=turns[:], func=ACT.Sin, scale=math.pi / 2)
+        cos_half = const.tile([P, H, T], F32)
+        nc.vector.tensor_mul(out=cos_half[:], in0=sin_quarter[:], in1=sin_quarter[:])
+        nc.vector.tensor_scalar(
+            out=cos_half[:], in0=cos_half[:], scalar1=-2.0, scalar2=1.0, op0=ALU.mult, op1=ALU.add
+        )
+        sin_x = const.tile([P, H, T], F32)
+        nc.vector.scalar_tensor_tensor(
+            out=sin_x[:], in0=sin_half[:], scalar=2.0, in1=cos_half[:], op0=ALU.mult, op1=ALU.mult
+        )
+        minus_sin_x = const.tile([P, H, T], F32)
+        nc.vector.tensor_scalar_mul(out=minus_sin_x[:], in0=sin_x[:], scalar1=-1.0)
+        cos_x = const.tile([P, H, T], F32)
+        nc.vector.tensor_mul(out=cos_x[:], in0=sin_half[:], in1=sin_half[:])
+        nc.vector.tensor_scalar(
+            out=cos_x[:], in0=cos_x[:], scalar1=-2.0, scalar2=1.0, op0=ALU.mult, op1=ALU.add
+        )
+        rotation = const.tile([P, 2, H * T, 2, 2], F32)
+        matrix = ((cos_x, minus_sin_x), (sin_x, cos_x))
+        for row in range(2):
+            for column in range(2):
+                entry = matrix[row][column][:].rearrange("p h t -> p (h t)")
+                nc.vector.tensor_copy(
+                    out=rotation[:, :, :, row, column],
+                    in_=entry.unsqueeze(1).to_broadcast([P, 2, H * T]),
+                )
+
+        sum_squares = const.tile([P, B, NARROW + WIDE], F32)
+        inverse = const.tile([P, B, NARROW + WIDE], F32)
+        with tc.psum_pool(name="flip_banks", bufs=4) as flip_banks, tc.psum_pool(
+            name="acc_banks", bufs=4
+        ) as acc_banks:
+            quantise(flip(w_rows, 0), nc.vector.tensor_copy, w_codes[:], w_scales[:])
+            quantise_batch(0)
+            for b in range(B):
+                if b + 1 < B:
+                    quantise_batch(b + 1)
+                gate = results.tile([P, H, T, DV], F32, tag="gate")
+                sq_narrow = work.tile([P, T, CHUNKS, DK], F32, tag="sq_narrow")
+                sq_wide = work.tile([P, T, H, DV], F32, tag="sq_wide")
+                for i in range(PAIRS):
+                    acc = project(acc_banks, b, i)
+                    two_tiles = slice(2 * i, 2 * i + 2)
+                    nc.scalar.activation(
+                        out=sq_narrow[:, two_tiles, :, :], in_=acc[:, :, :, 0:DK], func=ACT.Square
+                    )
+                    nc.scalar.activation(
+                        out=sq_wide[:, two_tiles, :, :], in_=acc[:, :, H:CHUNKS, DK:HEAD],
+                        func=ACT.Square,
+                    )
+                    nc.scalar.activation(
+                        out=gate[:, :, two_tiles, :].rearrange("p h j d -> p j h d"),
+                        in_=acc[:, :, 0:H, DK:HEAD], func=ACT.Silu,
+                    )
+                nc.scalar.activation(out=gate[:], in_=gate[:], func=ACT.Tanh)
+                nc.sync.dma_start(
+                    out=out_1[b].rearrange("h (p t) d -> p h (t d)", t=T),
+                    in_=gate[:].rearrange("p h t d -> p h (t d)"),
+                )
+                nc.vector.tensor_reduce(
+                    out=sum_squares[:, b, 0:NARROW],
+                    in_=sq_narrow[:].rearrange("p t c d -> p (t c) d"), axis=AXIS.X, op=ALU.add,
+                )
+                nc.vector.tensor_reduce(
+                    out=sum_squares[:, b, NARROW:],
+                    in_=sq_wide[:].rearrange("p t h d -> p (t h) d"), axis=AXIS.X, op=ALU.add,
+                )
+                nc.vector.tensor_scalar_max(
+                    out=sum_squares[:, b, :], in0=sum_squares[:, b, :], scalar1=EPS * EPS
+                )
+                nc.vector.reciprocal(out=inverse[:, b, :], in_=sum_squares[:, b, :])
+
+        inverse_norm = const.tile([P, B, NARROW + WIDE], F32)
+        nc.scalar.activation(out=inverse_norm[:], in_=inverse[:], func=ACT.Sqrt)
+
+        again_banks = ctx.enter_context(tc.psum_pool(name="again_banks", bufs=8))
+        for b in range(B):
+            qk = results.tile([P, CHUNKS, T, DK], F32, tag="qk")
+            v_n = results.tile([P, H, T, DV], F32, tag="v_n")
+            for i in range(PAIRS):
+                acc = project(again_banks, b, i)
+                two_tiles = slice(2 * i, 2 * i + 2)
+                narrow = inverse_norm[:, b, 2 * i * CHUNKS : (2 * i + 2) * CHUNKS]
+                wide = inverse_norm[:, b, NARROW + 2 * i * H : NARROW + (2 * i + 2) * H]
+                nc.vector.tensor_tensor(
+                    out=qk[:, :, two_tiles, :].rearrange("p c j d -> p j c d"),
+                    in0=acc[:, :, :, 0:DK],
+                    in1=narrow.rearrange("p (j c) -> p j c", j=2)
+                    .unsqueeze(3)
+                    .to_broadcast([P, 2, CHUNKS, DK]),
+                    op=ALU.mult,
+                )
+                nc.vector.tensor_tensor(
+                    out=v_n[:, :, two_tiles, :].rearrange("p h j d -> p j h d"),
+                    in0=acc[:, :, H:CHUNKS, DK:HEAD],
+                    in1=wide.rearrange("p (j h) -> p j h", j=2)
+                    .unsqueeze(3)
+                    .to_broadcast([P, 2, H, DV]),
+                    op=ALU.mult,
+                )
+            pair = qk[:].rearrange("p c t d -> p (c t) d")[:, :, 0:2]
+            products = work.tile([P, CHUNKS * T, 2, 2], F32, tag="products")
+            nc.vector.tensor_tensor(
+                out=products[:],
+                in0=pair.unsqueeze(2).to_broadcast([P, CHUNKS * T, 2, 2]),
+                in1=rotation[:].rearrange("p w g r c -> p (w g) r c"),
+                op=ALU.mult,
+            )
+            nc.vector.tensor_reduce(out=pair, in_=products[:], axis=AXIS.X, op=ALU.add)
+            nc.sync.dma_start(
+                out=out_0[b].rearrange("h (p t) d -> p h (t d)", t=T),
+                in_=qk[:, 0:H, :, :].rearrange("p h t d -> p h (t d)"),
+            )
+            nc.sync.dma_start(
+                out=out_2[b].rearrange("h (p t) d -> p h (t d)", t=T),
+                in_=qk[:, H:CHUNKS, :, :].rearrange("p h t d -> p h (t d)"),
+            )
+            nc.sync.dma_start(
+                out=out_3[b].rearrange("h (p t) d -> p h (t d)", t=T),
+                in_=v_n[:].rearrange("p h t d -> p h (t d)"),
+            )

@@ -6,7 +6,6 @@ from concourse.masks import make_identity
 
 F32 = mybir.dt.float32
 BF16 = mybir.dt.bfloat16
-I32 = mybir.dt.int32
 U32 = mybir.dt.uint32
 U8 = mybir.dt.uint8
 FP8X4 = mybir.dt.float8_e4m3fn_x4
@@ -24,10 +23,11 @@ EPS = 1e-12
 P = 128
 PACK = 4
 T = N // P
-PAIRS = T // 2
-WORDS = DIM // 2
-NARROW = T * CHUNKS
-WIDE = T * H
+HALF = T // 2
+HALVES = 2 * B
+BANKS = HALF // 2
+NARROW = HALF * CHUNKS
+WIDE = HALF * H
 
 ROUND_MAGIC = 1.5 * 2.0**23
 LOG_MAX = 6.0
@@ -40,22 +40,32 @@ def tile_gatedscreeningtile_pa_t_kernel(
 ):
     nc = tc.nc
     with ExitStack() as ctx:
+        ctx.enter_context(tc.manual_schedule())
         const = ctx.enter_context(tc.tile_pool(name="const", bufs=1))
         resident = ctx.enter_context(tc.tile_pool(name="resident", bufs=1))
-        stage = ctx.enter_context(tc.tile_pool(name="stage", bufs=4))
-        work = ctx.enter_context(tc.tile_pool(name="work", bufs=2))
-        results = ctx.enter_context(tc.tile_pool(name="results", bufs=3))
+        stage = ctx.enter_context(tc.tile_pool(name="stage", bufs=3))
+        results = ctx.enter_context(tc.tile_pool(name="results", bufs=4))
 
+        def live(h):
+            return 0 <= h < HALVES
+
+        def rows_of(dram, b):
+            return dram[b].rearrange("h (p t) d -> p h (t d)", t=T)
+
+        log_window = const.tile([P, H], BF16)
+        nc.scalar.dma_start(out=log_window[:], in_=sm_log.partition_broadcast(P))
         w_rows = const.tile([P, 2, DIM], BF16)
         nc.sync.dma_start(out=w_rows[:, 0, :], in_=w_qg)
         nc.sync.dma_start(out=w_rows[:, 1, :], in_=w_kv)
         x_rows = []
-        for b in range(B):
-            x_b = resident.tile([P, T, DIM], BF16, name="x_rows%d" % b)
-            nc.sync.dma_start(out=x_b[:], in_=tokens[b].rearrange("(p t) k -> p t k", t=T))
-            x_rows.append(x_b)
-        log_window = const.tile([P, H], BF16)
-        nc.sync.dma_start(out=log_window[:], in_=sm_log.partition_broadcast(P))
+        for h in range(HALVES):
+            x_h = resident.tile([P, HALF, DIM], BF16, name="x_rows%d" % h)
+            first = (h % 2) * HALF
+            nc.sync.dma_start(
+                out=x_h[:],
+                in_=tokens[h // 2].rearrange("(p t) k -> p t k", t=T)[:, first : first + HALF, :],
+            )
+            x_rows.append(x_h)
 
         warm = const.tile([P, 1], F32)
         nc.vector.memset(warm[:], 0.0)
@@ -64,58 +74,16 @@ def tile_gatedscreeningtile_pa_t_kernel(
         ident = const.tile([P, P], F32)
         make_identity(nc, ident[:])
 
-        def flip(rows, first):
-            words = rows[:].bitcast(F32)
-            flipped = flip_banks.tile([P, 2, 2, P], F32, tag="flipped")
-            for j in range(2):
-                for u in range(2):
-                    nc.tensor.transpose(
-                        flipped[:, j, u, :], words[:, first + j, u * P : (u + 1) * P], ident[:]
-                    )
-            return flipped
-
-        def quantise(flipped, copy, codes, scales):
-            grouped = stage.tile([P, 2 * P * PACK], BF16, tag="grouped", align_bytes=64)
-            copy(
-                out=grouped[:].bitcast(F32).rearrange("p (j r u) -> p j r u", j=2, u=2),
-                in_=flipped[:].rearrange("p j u r -> p j r u"),
-            )
-            nc.vector.quantize_mx(out=codes.bitcast(FP8X4), scales=scales, in_=grouped[:])
-
-        w_codes = const.tile([P, COLS], U32, align_bytes=64)
-        w_scales = const.tile([P, COLS], U8, align_bytes=64)
-
-        x_codes = []
-        x_scales = []
-        for b in range(B):
-            x_codes.append(resident.tile([P, T * P], U32, name="x_codes%d" % b, align_bytes=64))
-            x_scales.append(resident.tile([P, T * P], U8, name="x_scales%d" % b, align_bytes=64))
-
-        def quantise_batch(b):
-            flipped = [flip(x_rows[b], 2 * i) for i in range(PAIRS)]
-            for i in range(PAIRS):
-                copy = nc.scalar.copy if i % 2 == 0 else nc.vector.tensor_copy
-                cols = slice(2 * i * P, (2 * i + 2) * P)
-                quantise(flipped[i], copy, x_codes[b][:, cols], x_scales[b][:, cols])
-
-        def project(banks, b, i):
-            acc = banks.tile([P, 2, COLS], F32, tag="acc")
-            for j in range(2):
-                cols = slice((2 * i + j) * P, (2 * i + j + 1) * P)
-                nc.tensor.matmul_mx(
-                    out=acc[:, j, :],
-                    lhsT=x_codes[b][:, cols].bitcast(FP8X4),
-                    lhsT_scale=x_scales[b][:, cols],
-                    rhs=w_codes[:].bitcast(FP8X4),
-                    rhs_scale=w_scales[:],
-                    start=True,
-                    stop=True,
-                )
-            return acc[:].rearrange("p j (c d) -> p j c d", d=HEAD)
-
-        window = const.tile([P, H], F32)
         two = const.tile([P, H], F32)
+        minus_one = const.tile([P, H], F32)
+        position = const.tile([P, T], F32)
+        window = const.tile([P, H], F32)
         nc.gpsimd.memset(two[:], 2.0)
+        nc.gpsimd.memset(minus_one[:], -1.0)
+        nc.gpsimd.iota(
+            position[:], pattern=[[1, T]], base=0, channel_multiplier=T,
+            allow_small_or_imprecise_dtypes=True,
+        )
         nc.gpsimd.tensor_scalar(
             out=window[:], in0=log_window[:], scalar1=LOG_MAX, scalar2=1.0 / math.log(2.0),
             op0=ALU.min, op1=ALU.mult,
@@ -129,148 +97,253 @@ def tile_gatedscreeningtile_pa_t_kernel(
             out=cos_window[:], in_=window[:], func=ACT.Sin, scale=-math.pi / WT, bias=math.pi / 2
         )
         per_position = const.tile([P, H], F32)
-        nc.vector.reciprocal(out=per_position[:], in_=window[:])
-        nc.vector.scalar_tensor_tensor(
-            out=per_position[:], in0=cos_window[:], scalar=1.0, in1=per_position[:],
-            op0=ALU.add, op1=ALU.mult,
-        )
-        position_int = const.tile([P, T], I32)
-        nc.gpsimd.iota(position_int[:], pattern=[[1, T]], base=0, channel_multiplier=T)
-        position = const.tile([P, T], F32)
-        nc.vector.tensor_copy(out=position[:], in_=position_int[:])
+        nc.gpsimd.tensor_tensor(out=per_position[:], in0=window[:], in1=minus_one[:], op=ALU.pow)
+        nc.gpsimd.tensor_scalar_add(out=cos_window[:], in0=cos_window[:], scalar1=1.0)
+        nc.gpsimd.tensor_mul(out=per_position[:], in0=per_position[:], in1=cos_window[:])
         turns = const.tile([P, H, T], F32)
-        for h in range(H):
-            nc.vector.tensor_scalar(
-                out=turns[:, h, :], in0=position[:], scalar1=per_position[:, h : h + 1],
-                scalar2=0.25, op0=ALU.mult, op1=ALU.mult,
+        for head in range(H):
+            nc.gpsimd.tensor_scalar(
+                out=turns[:, head, :], in0=position[:],
+                scalar1=per_position[:, head : head + 1], scalar2=0.25,
+                op0=ALU.mult, op1=ALU.mult,
             )
         whole = const.tile([P, H, T], F32)
-        nc.vector.tensor_scalar(
+        nc.gpsimd.tensor_scalar(
             out=whole[:], in0=turns[:], scalar1=ROUND_MAGIC, scalar2=ROUND_MAGIC,
             op0=ALU.add, op1=ALU.subtract,
         )
-        nc.vector.tensor_sub(out=turns[:], in0=turns[:], in1=whole[:])
-        sin_half = const.tile([P, H, T], F32)
-        sin_quarter = const.tile([P, H, T], F32)
-        nc.scalar.activation(out=sin_half[:], in_=turns[:], func=ACT.Sin, scale=math.pi)
-        nc.scalar.activation(out=sin_quarter[:], in_=turns[:], func=ACT.Sin, scale=math.pi / 2)
-        cos_half = const.tile([P, H, T], F32)
-        nc.vector.tensor_mul(out=cos_half[:], in0=sin_quarter[:], in1=sin_quarter[:])
-        nc.vector.tensor_scalar(
-            out=cos_half[:], in0=cos_half[:], scalar1=-2.0, scalar2=1.0, op0=ALU.mult, op1=ALU.add
-        )
-        sin_x = const.tile([P, H, T], F32)
-        nc.vector.scalar_tensor_tensor(
-            out=sin_x[:], in0=sin_half[:], scalar=2.0, in1=cos_half[:], op0=ALU.mult, op1=ALU.mult
-        )
-        minus_sin_x = const.tile([P, H, T], F32)
-        nc.vector.tensor_scalar_mul(out=minus_sin_x[:], in0=sin_x[:], scalar1=-1.0)
-        cos_x = const.tile([P, H, T], F32)
-        nc.vector.tensor_mul(out=cos_x[:], in0=sin_half[:], in1=sin_half[:])
-        nc.vector.tensor_scalar(
-            out=cos_x[:], in0=cos_x[:], scalar1=-2.0, scalar2=1.0, op0=ALU.mult, op1=ALU.add
-        )
-        rotation = const.tile([P, 2, H * T, 2, 2], F32)
-        matrix = ((cos_x, minus_sin_x), (sin_x, cos_x))
-        for row in range(2):
-            for column in range(2):
-                entry = matrix[row][column][:].rearrange("p h t -> p (h t)")
-                nc.vector.tensor_copy(
-                    out=rotation[:, :, :, row, column],
-                    in_=entry.unsqueeze(1).to_broadcast([P, 2, H * T]),
-                )
+        nc.gpsimd.tensor_sub(out=turns[:], in0=turns[:], in1=whole[:])
 
-        sum_squares = const.tile([P, B, NARROW + WIDE], F32)
-        inverse = const.tile([P, B, NARROW + WIDE], F32)
+        def finish_rotation_table():
+            sin_half = const.tile([P, H * T], F32)
+            sin_quarter = const.tile([P, H * T], F32)
+            flat_turns = turns[:].rearrange("p h t -> p (h t)")
+            nc.scalar.activation(out=sin_half[:], in_=flat_turns, func=ACT.Sin, scale=math.pi)
+            nc.scalar.activation(
+                out=sin_quarter[:], in_=flat_turns, func=ACT.Sin, scale=math.pi / 2
+            )
+            cos_half = const.tile([P, H * T], F32)
+            nc.gpsimd.tensor_mul(out=cos_half[:], in0=sin_quarter[:], in1=sin_quarter[:])
+            nc.gpsimd.tensor_scalar(
+                out=cos_half[:], in0=cos_half[:], scalar1=-2.0, scalar2=1.0,
+                op0=ALU.mult, op1=ALU.add,
+            )
+            half_sin_x = const.tile([P, H * T], F32)
+            nc.gpsimd.tensor_mul(out=half_sin_x[:], in0=sin_half[:], in1=cos_half[:])
+            sin_half_squared = const.tile([P, H * T], F32)
+            nc.gpsimd.tensor_mul(out=sin_half_squared[:], in0=sin_half[:], in1=sin_half[:])
+            table = const.tile([P, 2, H * T, 2, 2], F32, name="rotation")
+            for_q_and_k = [P, 2, H * T]
+            for diagonal in range(2):
+                nc.gpsimd.tensor_scalar(
+                    out=table[:, :, :, diagonal, diagonal],
+                    in0=sin_half_squared[:].unsqueeze(1).to_broadcast(for_q_and_k),
+                    scalar1=-2.0, scalar2=1.0, op0=ALU.mult, op1=ALU.add,
+                )
+            nc.gpsimd.tensor_scalar_mul(
+                out=table[:, :, :, 0, 1],
+                in0=half_sin_x[:].unsqueeze(1).to_broadcast(for_q_and_k), scalar1=-2.0,
+            )
+            nc.gpsimd.tensor_scalar_mul(
+                out=table[:, :, :, 1, 0],
+                in0=half_sin_x[:].unsqueeze(1).to_broadcast(for_q_and_k), scalar1=2.0,
+            )
+            return table
+
+        def flip(banks, rows, first):
+            words = rows[:].bitcast(F32)
+            flipped = banks.tile([P, 2, 2, P], F32, tag="flipped")
+            for j in range(2):
+                for u in range(2):
+                    nc.tensor.transpose(
+                        flipped[:, j, u, :], words[:, first + j, u * P : (u + 1) * P], ident[:]
+                    )
+            return flipped
+
+        def regroup(copy, flipped, grouped):
+            copy(
+                out=grouped.bitcast(F32).rearrange("p (j r u) -> p j r u", j=2, u=2),
+                in_=flipped[:].rearrange("p j u r -> p j r u"),
+            )
+
+        BANK_COLS = 2 * P * PACK
+        w_codes = const.tile([P, COLS], U32, align_bytes=64)
+        w_scales = const.tile([P, COLS], U8, align_bytes=64)
+        x_codes = []
+        x_scales = []
+        for h in range(HALVES):
+            x_codes.append(resident.tile([P, HALF * P], U32, name="x_codes%d" % h, align_bytes=64))
+            x_scales.append(resident.tile([P, HALF * P], U8, name="x_scales%d" % h, align_bytes=64))
+
+        def project(banks, h):
+            products = []
+            for i in range(BANKS):
+                acc = banks.tile([P, 2, COLS], F32, tag="acc")
+                for j in range(2):
+                    cols = slice((2 * i + j) * P, (2 * i + j + 1) * P)
+                    nc.tensor.matmul_mx(
+                        out=acc[:, j, :],
+                        lhsT=x_codes[h][:, cols].bitcast(FP8X4),
+                        lhsT_scale=x_scales[h][:, cols],
+                        rhs=w_codes[:].bitcast(FP8X4),
+                        rhs_scale=w_scales[:],
+                        start=True,
+                        stop=True,
+                    )
+                products.append(acc[:].rearrange("p j (c d) -> p j c d", d=HEAD))
+            return products
+
+        sum_squares = const.tile([P, HALVES, NARROW + WIDE], F32)
+        inverse = const.tile([P, HALVES, NARROW + WIDE], F32)
+        flipped_of = {}
+        grouped_of = {}
+        acc_of = {}
+        squares_of = {}
+        gate_of = {}
+
         with tc.psum_pool(name="flip_banks", bufs=4) as flip_banks, tc.psum_pool(
             name="acc_banks", bufs=4
         ) as acc_banks:
-            quantise(flip(w_rows, 0), nc.vector.tensor_copy, w_codes[:], w_scales[:])
-            quantise_batch(0)
-            for b in range(B):
-                if b + 1 < B:
-                    quantise_batch(b + 1)
-                gate = results.tile([P, H, T, DV], F32, tag="gate")
-                sq_narrow = work.tile([P, T, CHUNKS, DK], F32, tag="sq_narrow")
-                sq_wide = work.tile([P, T, H, DV], F32, tag="sq_wide")
-                for i in range(PAIRS):
-                    acc = project(acc_banks, b, i)
-                    two_tiles = slice(2 * i, 2 * i + 2)
-                    nc.scalar.activation(
-                        out=sq_narrow[:, two_tiles, :, :], in_=acc[:, :, :, 0:DK], func=ACT.Square
-                    )
-                    nc.scalar.activation(
-                        out=sq_wide[:, two_tiles, :, :], in_=acc[:, :, H:CHUNKS, DK:HEAD],
-                        func=ACT.Square,
-                    )
-                    nc.scalar.activation(
-                        out=gate[:, :, two_tiles, :].rearrange("p h j d -> p j h d"),
-                        in_=acc[:, :, 0:H, DK:HEAD], func=ACT.Silu,
-                    )
-                nc.scalar.activation(out=gate[:], in_=gate[:], func=ACT.Tanh)
-                nc.sync.dma_start(
-                    out=out_1[b].rearrange("h (p t) d -> p h (t d)", t=T),
-                    in_=gate[:].rearrange("p h t d -> p h (t d)"),
-                )
-                nc.vector.tensor_reduce(
-                    out=sum_squares[:, b, 0:NARROW],
-                    in_=sq_narrow[:].rearrange("p t c d -> p (t c) d"), axis=AXIS.X, op=ALU.add,
-                )
-                nc.vector.tensor_reduce(
-                    out=sum_squares[:, b, NARROW:],
-                    in_=sq_wide[:].rearrange("p t h d -> p (t h) d"), axis=AXIS.X, op=ALU.add,
-                )
-                nc.vector.tensor_scalar_max(
-                    out=sum_squares[:, b, :], in0=sum_squares[:, b, :], scalar1=EPS * EPS
-                )
-                nc.vector.reciprocal(out=inverse[:, b, :], in_=sum_squares[:, b, :])
+            w_grouped = const.tile([P, BANK_COLS], BF16, align_bytes=64)
+            regroup(nc.vector.tensor_copy, flip(flip_banks, w_rows, 0), w_grouped[:])
+            nc.vector.quantize_mx(
+                out=w_codes[:].bitcast(FP8X4), scales=w_scales[:], in_=w_grouped[:]
+            )
 
-        inverse_norm = const.tile([P, B, NARROW + WIDE], F32)
+            def first_sweep_step(h):
+                if live(h + 1):
+                    nc.vector.quantize_mx(
+                        out=x_codes[h + 1][:].bitcast(FP8X4), scales=x_scales[h + 1][:],
+                        in_=grouped_of[h + 1][:],
+                    )
+                    acc_of[h + 1] = project(acc_banks, h + 1)
+                if live(h + 3):
+                    flipped_of[h + 3] = [
+                        flip(flip_banks, x_rows[h + 3], 2 * i) for i in range(BANKS)
+                    ]
+                if live(h - 2):
+                    nc.vector.tensor_scalar_max(
+                        out=sum_squares[:, h - 2, :], in0=sum_squares[:, h - 2, :],
+                        scalar1=EPS * EPS,
+                    )
+                if live(h):
+                    if h % 2 == 0:
+                        gate_of[h // 2] = results.tile([P, H, T, DV], F32, name="gate", tag="gate")
+                    gate = gate_of[h // 2]
+                    sq_narrow = stage.tile([P, HALF, CHUNKS, DK], F32, tag="sq_narrow")
+                    sq_wide = stage.tile([P, HALF, H, DV], F32, tag="sq_wide")
+                    squares_of[h] = (sq_narrow, sq_wide)
+                    for i in range(BANKS):
+                        acc = acc_of[h][i]
+                        here = slice(2 * i, 2 * i + 2)
+                        there = slice((h % 2) * HALF + 2 * i, (h % 2) * HALF + 2 * i + 2)
+                        nc.scalar.activation(
+                            out=sq_narrow[:, here, :, :], in_=acc[:, :, :, 0:DK], func=ACT.Square
+                        )
+                        nc.scalar.activation(
+                            out=sq_wide[:, here, :, :], in_=acc[:, :, H:CHUNKS, DK:HEAD],
+                            func=ACT.Square,
+                        )
+                        nc.scalar.activation(
+                            out=gate[:, :, there, :].rearrange("p h j d -> p j h d"),
+                            in_=acc[:, :, 0:H, DK:HEAD], func=ACT.Silu,
+                        )
+                if live(h + 2):
+                    grouped = stage.tile([P, BANKS * BANK_COLS], BF16, tag="grouped", align_bytes=64)
+                    grouped_of[h + 2] = grouped
+                    regroup(nc.scalar.copy, flipped_of[h + 2][0], grouped[:, 0:BANK_COLS])
+                    regroup(nc.vector.tensor_copy, flipped_of[h + 2][1], grouped[:, BANK_COLS:])
+                if live(h - 2):
+                    nc.vector.reciprocal(out=inverse[:, h - 2, :], in_=sum_squares[:, h - 2, :])
+                if live(h - 1):
+                    sq_narrow, sq_wide = squares_of[h - 1]
+                    nc.vector.tensor_reduce(
+                        out=sum_squares[:, h - 1, 0:NARROW],
+                        in_=sq_narrow[:].rearrange("p t c d -> p (t c) d"), axis=AXIS.X, op=ALU.add,
+                    )
+                    nc.vector.tensor_reduce(
+                        out=sum_squares[:, h - 1, NARROW:],
+                        in_=sq_wide[:].rearrange("p t h d -> p (t h) d"), axis=AXIS.X, op=ALU.add,
+                    )
+                    gate = gate_of[(h - 1) // 2]
+                    there = slice(((h - 1) % 2) * HALF, ((h - 1) % 2 + 1) * HALF)
+                    nc.scalar.activation(
+                        out=gate[:, :, there, :], in_=gate[:, :, there, :], func=ACT.Tanh
+                    )
+                    if (h - 1) % 2 == 1:
+                        nc.sync.dma_start(
+                            out=rows_of(out_1, (h - 1) // 2),
+                            in_=gate[:].rearrange("p h t d -> p h (t d)"),
+                        )
+
+            for h in range(-3, HALVES // 2):
+                first_sweep_step(h)
+            rotation = finish_rotation_table()
+            for h in range(HALVES // 2, HALVES + 2):
+                first_sweep_step(h)
+
+        inverse_norm = const.tile([P, HALVES, NARROW + WIDE], F32)
         nc.scalar.activation(out=inverse_norm[:], in_=inverse[:], func=ACT.Sqrt)
 
         again_banks = ctx.enter_context(tc.psum_pool(name="again_banks", bufs=8))
-        for b in range(B):
-            qk = results.tile([P, CHUNKS, T, DK], F32, tag="qk")
-            v_n = results.tile([P, H, T, DV], F32, tag="v_n")
-            for i in range(PAIRS):
-                acc = project(again_banks, b, i)
-                two_tiles = slice(2 * i, 2 * i + 2)
-                narrow = inverse_norm[:, b, 2 * i * CHUNKS : (2 * i + 2) * CHUNKS]
-                wide = inverse_norm[:, b, NARROW + 2 * i * H : NARROW + (2 * i + 2) * H]
+        AHEAD = 2
+        qk_of = {}
+        v_of = {}
+        rotated_of = {}
+        for h in range(AHEAD):
+            acc_of[h] = project(again_banks, h)
+        for h in range(HALVES + 1):
+            b = h // 2
+            if live(h + AHEAD):
+                acc_of[h + AHEAD] = project(again_banks, h + AHEAD)
+            if live(h):
+                if h % 2 == 0:
+                    qk_of[b] = results.tile([P, CHUNKS, T, DK], F32, name="qk", tag="qk")
+                    v_of[b] = results.tile([P, H, T, DV], F32, name="v_n", tag="v_n")
+                for i in range(BANKS):
+                    there = slice((h % 2) * HALF + 2 * i, (h % 2) * HALF + 2 * i + 2)
+                    narrow = inverse_norm[:, h, 2 * i * CHUNKS : (2 * i + 2) * CHUNKS]
+                    nc.vector.tensor_tensor(
+                        out=qk_of[b][:, :, there, :].rearrange("p c j d -> p j c d"),
+                        in0=acc_of[h][i][:, :, :, 0:DK],
+                        in1=narrow.rearrange("p (j c) -> p j c", j=2)
+                        .unsqueeze(3)
+                        .to_broadcast([P, 2, CHUNKS, DK]),
+                        op=ALU.mult,
+                    )
+            if h % 2 == 0 and h > 0:
+                pair, products = rotated_of[b - 1]
+                nc.vector.tensor_reduce(out=pair, in_=products[:], axis=AXIS.X, op=ALU.add)
+                nc.sync.dma_start(
+                    out=rows_of(out_0, b - 1),
+                    in_=qk_of[b - 1][:, 0:H, :, :].rearrange("p h t d -> p h (t d)"),
+                )
+                nc.sync.dma_start(
+                    out=rows_of(out_2, b - 1),
+                    in_=qk_of[b - 1][:, H:CHUNKS, :, :].rearrange("p h t d -> p h (t d)"),
+                )
+            if live(h):
+                for i in range(BANKS):
+                    there = slice((h % 2) * HALF + 2 * i, (h % 2) * HALF + 2 * i + 2)
+                    wide = inverse_norm[:, h, NARROW + 2 * i * H : NARROW + (2 * i + 2) * H]
+                    nc.vector.tensor_tensor(
+                        out=v_of[b][:, :, there, :].rearrange("p h j d -> p j h d"),
+                        in0=acc_of[h][i][:, :, H:CHUNKS, DK:HEAD],
+                        in1=wide.rearrange("p (j h) -> p j h", j=2)
+                        .unsqueeze(3)
+                        .to_broadcast([P, 2, H, DV]),
+                        op=ALU.mult,
+                    )
+            if live(h) and h % 2 == 1:
+                nc.sync.dma_start(
+                    out=rows_of(out_3, b), in_=v_of[b][:].rearrange("p h t d -> p h (t d)")
+                )
+                pair = qk_of[b][:].rearrange("p c t d -> p (c t) d")[:, :, 0:2]
+                products = stage.tile([P, CHUNKS * T, 2, 2], F32, tag="products")
                 nc.vector.tensor_tensor(
-                    out=qk[:, :, two_tiles, :].rearrange("p c j d -> p j c d"),
-                    in0=acc[:, :, :, 0:DK],
-                    in1=narrow.rearrange("p (j c) -> p j c", j=2)
-                    .unsqueeze(3)
-                    .to_broadcast([P, 2, CHUNKS, DK]),
+                    out=products[:],
+                    in0=pair.unsqueeze(2).to_broadcast([P, CHUNKS * T, 2, 2]),
+                    in1=rotation[:].rearrange("p w g r c -> p (w g) r c"),
                     op=ALU.mult,
                 )
-                nc.vector.tensor_tensor(
-                    out=v_n[:, :, two_tiles, :].rearrange("p h j d -> p j h d"),
-                    in0=acc[:, :, H:CHUNKS, DK:HEAD],
-                    in1=wide.rearrange("p (j h) -> p j h", j=2)
-                    .unsqueeze(3)
-                    .to_broadcast([P, 2, H, DV]),
-                    op=ALU.mult,
-                )
-            pair = qk[:].rearrange("p c t d -> p (c t) d")[:, :, 0:2]
-            products = work.tile([P, CHUNKS * T, 2, 2], F32, tag="products")
-            nc.vector.tensor_tensor(
-                out=products[:],
-                in0=pair.unsqueeze(2).to_broadcast([P, CHUNKS * T, 2, 2]),
-                in1=rotation[:].rearrange("p w g r c -> p (w g) r c"),
-                op=ALU.mult,
-            )
-            nc.vector.tensor_reduce(out=pair, in_=products[:], axis=AXIS.X, op=ALU.add)
-            nc.sync.dma_start(
-                out=out_0[b].rearrange("h (p t) d -> p h (t d)", t=T),
-                in_=qk[:, 0:H, :, :].rearrange("p h t d -> p h (t d)"),
-            )
-            nc.sync.dma_start(
-                out=out_2[b].rearrange("h (p t) d -> p h (t d)", t=T),
-                in_=qk[:, H:CHUNKS, :, :].rearrange("p h t d -> p h (t d)"),
-            )
-            nc.sync.dma_start(
-                out=out_3[b].rearrange("h (p t) d -> p h (t d)", t=T),
-                in_=v_n[:].rearrange("p h t d -> p h (t d)"),
-            )
+                rotated_of[b] = (pair, products)

@@ -31,6 +31,7 @@ WIDE = HALF * H
 
 ROUND_MAGIC = 1.5 * 2.0**23
 LOG_MAX = 6.0
+SUM_LAG = 4
 
 FLOPS = 2 * B * N * DIM * COLS
 
@@ -44,6 +45,7 @@ def tile_gatedscreeningtile_pa_t_kernel(
         const = ctx.enter_context(tc.tile_pool(name="const", bufs=1))
         resident = ctx.enter_context(tc.tile_pool(name="resident", bufs=1))
         stage = ctx.enter_context(tc.tile_pool(name="stage", bufs=3))
+        squares = ctx.enter_context(tc.tile_pool(name="squares", bufs=SUM_LAG + 2))
         results = ctx.enter_context(tc.tile_pool(name="results", bufs=4))
 
         def live(h):
@@ -194,7 +196,6 @@ def tile_gatedscreeningtile_pa_t_kernel(
             return products
 
         sum_squares = const.tile([P, HALVES, NARROW + WIDE], F32)
-        inverse = const.tile([P, HALVES, NARROW + WIDE], F32)
         flipped_of = {}
         grouped_of = {}
         acc_of = {}
@@ -221,17 +222,17 @@ def tile_gatedscreeningtile_pa_t_kernel(
                     flipped_of[h + 3] = [
                         flip(flip_banks, x_rows[h + 3], 2 * i) for i in range(BANKS)
                     ]
-                if live(h - 2):
+                if live(h - SUM_LAG - 1):
                     nc.vector.tensor_scalar_max(
-                        out=sum_squares[:, h - 2, :], in0=sum_squares[:, h - 2, :],
-                        scalar1=EPS * EPS,
+                        out=sum_squares[:, h - SUM_LAG - 1, :],
+                        in0=sum_squares[:, h - SUM_LAG - 1, :], scalar1=EPS * EPS,
                     )
                 if live(h):
                     if h % 2 == 0:
                         gate_of[h // 2] = results.tile([P, H, T, DV], F32, name="gate", tag="gate")
                     gate = gate_of[h // 2]
-                    sq_narrow = stage.tile([P, HALF, CHUNKS, DK], F32, tag="sq_narrow")
-                    sq_wide = stage.tile([P, HALF, H, DV], F32, tag="sq_wide")
+                    sq_narrow = squares.tile([P, HALF, CHUNKS, DK], F32, tag="sq_narrow")
+                    sq_wide = squares.tile([P, HALF, H, DV], F32, tag="sq_wide")
                     squares_of[h] = (sq_narrow, sq_wide)
                     for i in range(BANKS):
                         acc = acc_of[h][i]
@@ -251,20 +252,20 @@ def tile_gatedscreeningtile_pa_t_kernel(
                 if live(h + 2):
                     grouped = stage.tile([P, BANKS * BANK_COLS], BF16, tag="grouped", align_bytes=64)
                     grouped_of[h + 2] = grouped
-                    regroup(nc.scalar.copy, flipped_of[h + 2][0], grouped[:, 0:BANK_COLS])
+                    first_copy = nc.scalar.copy if h % 2 == 0 else nc.vector.tensor_copy
+                    regroup(first_copy, flipped_of[h + 2][0], grouped[:, 0:BANK_COLS])
                     regroup(nc.vector.tensor_copy, flipped_of[h + 2][1], grouped[:, BANK_COLS:])
-                if live(h - 2):
-                    nc.vector.reciprocal(out=inverse[:, h - 2, :], in_=sum_squares[:, h - 2, :])
-                if live(h - 1):
-                    sq_narrow, sq_wide = squares_of[h - 1]
+                if live(h - SUM_LAG):
+                    sq_narrow, sq_wide = squares_of[h - SUM_LAG]
                     nc.vector.tensor_reduce(
-                        out=sum_squares[:, h - 1, 0:NARROW],
+                        out=sum_squares[:, h - SUM_LAG, 0:NARROW],
                         in_=sq_narrow[:].rearrange("p t c d -> p (t c) d"), axis=AXIS.X, op=ALU.add,
                     )
                     nc.vector.tensor_reduce(
-                        out=sum_squares[:, h - 1, NARROW:],
+                        out=sum_squares[:, h - SUM_LAG, NARROW:],
                         in_=sq_wide[:].rearrange("p t h d -> p (t h) d"), axis=AXIS.X, op=ALU.add,
                     )
+                if live(h - 1):
                     gate = gate_of[(h - 1) // 2]
                     there = slice(((h - 1) % 2) * HALF, ((h - 1) % 2 + 1) * HALF)
                     nc.scalar.activation(
@@ -279,11 +280,15 @@ def tile_gatedscreeningtile_pa_t_kernel(
             for h in range(-3, HALVES // 2):
                 first_sweep_step(h)
             rotation = finish_rotation_table()
-            for h in range(HALVES // 2, HALVES + 2):
+            for h in range(HALVES // 2, HALVES + SUM_LAG + 2):
                 first_sweep_step(h)
 
         inverse_norm = const.tile([P, HALVES, NARROW + WIDE], F32)
-        nc.scalar.activation(out=inverse_norm[:], in_=inverse[:], func=ACT.Sqrt)
+        for part in (slice(0, HALVES // 2), slice(HALVES // 2, HALVES)):
+            nc.scalar.activation(
+                out=inverse_norm[:, part, :], in_=sum_squares[:, part, :],
+                func=ACT.Abs_reciprocal_sqrt,
+            )
 
         again_banks = ctx.enter_context(tc.psum_pool(name="again_banks", bufs=8))
         AHEAD = 2

@@ -31,7 +31,7 @@ WIDE = HALF * H
 
 ROUND_MAGIC = 1.5 * 2.0**23
 LOG_MAX = 6.0
-SUM_LAG = 4
+SUM_LAG = 2
 
 FLOPS = 2 * B * N * DIM * COLS
 
@@ -212,16 +212,16 @@ def tile_gatedscreeningtile_pa_t_kernel(
             )
 
             def first_sweep_step(h):
+                if live(h + 3):
+                    flipped_of[h + 3] = [
+                        flip(flip_banks, x_rows[h + 3], 2 * i) for i in range(BANKS)
+                    ]
                 if live(h + 1):
                     nc.vector.quantize_mx(
                         out=x_codes[h + 1][:].bitcast(FP8X4), scales=x_scales[h + 1][:],
                         in_=grouped_of[h + 1][:],
                     )
                     acc_of[h + 1] = project(acc_banks, h + 1)
-                if live(h + 3):
-                    flipped_of[h + 3] = [
-                        flip(flip_banks, x_rows[h + 3], 2 * i) for i in range(BANKS)
-                    ]
                 if live(h - SUM_LAG - 1):
                     nc.vector.tensor_scalar_max(
                         out=sum_squares[:, h - SUM_LAG - 1, :],
@@ -292,63 +292,58 @@ def tile_gatedscreeningtile_pa_t_kernel(
 
         again_banks = ctx.enter_context(tc.psum_pool(name="again_banks", bufs=8))
         AHEAD = 2
-        qk_of = {}
-        v_of = {}
-        rotated_of = {}
         for h in range(AHEAD):
             acc_of[h] = project(again_banks, h)
-        for h in range(HALVES + 1):
+        for h in range(HALVES):
             b = h // 2
             if live(h + AHEAD):
                 acc_of[h + AHEAD] = project(again_banks, h + AHEAD)
-            if live(h):
-                if h % 2 == 0:
-                    qk_of[b] = results.tile([P, CHUNKS, T, DK], F32, name="qk", tag="qk")
-                    v_of[b] = results.tile([P, H, T, DV], F32, name="v_n", tag="v_n")
-                for i in range(BANKS):
-                    there = slice((h % 2) * HALF + 2 * i, (h % 2) * HALF + 2 * i + 2)
-                    narrow = inverse_norm[:, h, 2 * i * CHUNKS : (2 * i + 2) * CHUNKS]
-                    nc.vector.tensor_tensor(
-                        out=qk_of[b][:, :, there, :].rearrange("p c j d -> p j c d"),
-                        in0=acc_of[h][i][:, :, :, 0:DK],
-                        in1=narrow.rearrange("p (j c) -> p j c", j=2)
-                        .unsqueeze(3)
-                        .to_broadcast([P, 2, CHUNKS, DK]),
-                        op=ALU.mult,
-                    )
-            if h % 2 == 0 and h > 0:
-                pair, products = rotated_of[b - 1]
-                nc.vector.tensor_reduce(out=pair, in_=products[:], axis=AXIS.X, op=ALU.add)
-                nc.sync.dma_start(
-                    out=rows_of(out_0, b - 1),
-                    in_=qk_of[b - 1][:, 0:H, :, :].rearrange("p h t d -> p h (t d)"),
-                )
-                nc.sync.dma_start(
-                    out=rows_of(out_2, b - 1),
-                    in_=qk_of[b - 1][:, H:CHUNKS, :, :].rearrange("p h t d -> p h (t d)"),
-                )
-            if live(h):
-                for i in range(BANKS):
-                    there = slice((h % 2) * HALF + 2 * i, (h % 2) * HALF + 2 * i + 2)
-                    wide = inverse_norm[:, h, NARROW + 2 * i * H : NARROW + (2 * i + 2) * H]
-                    nc.vector.tensor_tensor(
-                        out=v_of[b][:, :, there, :].rearrange("p h j d -> p j h d"),
-                        in0=acc_of[h][i][:, :, H:CHUNKS, DK:HEAD],
-                        in1=wide.rearrange("p (j h) -> p j h", j=2)
-                        .unsqueeze(3)
-                        .to_broadcast([P, 2, H, DV]),
-                        op=ALU.mult,
-                    )
-            if live(h) and h % 2 == 1:
-                nc.sync.dma_start(
-                    out=rows_of(out_3, b), in_=v_of[b][:].rearrange("p h t d -> p h (t d)")
-                )
-                pair = qk_of[b][:].rearrange("p c t d -> p (c t) d")[:, :, 0:2]
-                products = stage.tile([P, CHUNKS * T, 2, 2], F32, tag="products")
+            if h % 2 == 0:
+                qk = results.tile([P, CHUNKS, T, DK], F32, tag="qk")
+                v_n = results.tile([P, H, T, DV], F32, tag="v_n")
+            for i in range(BANKS):
+                there = slice((h % 2) * HALF + 2 * i, (h % 2) * HALF + 2 * i + 2)
+                narrow = inverse_norm[:, h, 2 * i * CHUNKS : (2 * i + 2) * CHUNKS]
                 nc.vector.tensor_tensor(
+                    out=qk[:, :, there, :].rearrange("p c j d -> p j c d"),
+                    in0=acc_of[h][i][:, :, :, 0:DK],
+                    in1=narrow.rearrange("p (j c) -> p j c", j=2)
+                    .unsqueeze(3)
+                    .to_broadcast([P, 2, CHUNKS, DK]),
+                    op=ALU.mult,
+                )
+            if h % 2 == 1:
+                pair = qk[:].rearrange("p c t d -> p (c t) d")[:, :, 0:2]
+                products = stage.tile([P, CHUNKS * T, 2, 2], F32, tag="products")
+                nc.gpsimd.tensor_tensor(
                     out=products[:],
                     in0=pair.unsqueeze(2).to_broadcast([P, CHUNKS * T, 2, 2]),
                     in1=rotation[:].rearrange("p w g r c -> p (w g) r c"),
                     op=ALU.mult,
                 )
-                rotated_of[b] = (pair, products)
+                nc.gpsimd.tensor_add(
+                    out=pair, in0=products[:, :, :, 0], in1=products[:, :, :, 1]
+                )
+            for i in range(BANKS):
+                there = slice((h % 2) * HALF + 2 * i, (h % 2) * HALF + 2 * i + 2)
+                wide = inverse_norm[:, h, NARROW + 2 * i * H : NARROW + (2 * i + 2) * H]
+                nc.vector.tensor_tensor(
+                    out=v_n[:, :, there, :].rearrange("p h j d -> p j h d"),
+                    in0=acc_of[h][i][:, :, H:CHUNKS, DK:HEAD],
+                    in1=wide.rearrange("p (j h) -> p j h", j=2)
+                    .unsqueeze(3)
+                    .to_broadcast([P, 2, H, DV]),
+                    op=ALU.mult,
+                )
+            if h % 2 == 1:
+                nc.sync.dma_start(
+                    out=rows_of(out_3, b), in_=v_n[:].rearrange("p h t d -> p h (t d)")
+                )
+                nc.sync.dma_start(
+                    out=rows_of(out_0, b),
+                    in_=qk[:, 0:H, :, :].rearrange("p h t d -> p h (t d)"),
+                )
+                nc.sync.dma_start(
+                    out=rows_of(out_2, b),
+                    in_=qk[:, H:CHUNKS, :, :].rearrange("p h t d -> p h (t d)"),
+                )

import math
from contextlib import ExitStack

import concourse.mybir as mybir
from concourse.masks import make_identity

F32 = mybir.dt.float32
BF16 = mybir.dt.bfloat16
U32 = mybir.dt.uint32
U8 = mybir.dt.uint8
FP8X4 = mybir.dt.float8_e4m3fn_x4
ACT = mybir.ActivationFunctionType
ALU = mybir.AluOpType
AXIS = mybir.AxisListType

B, N, DIM, H, DK, DV = 8, 1024, 512, 2, 16, 48
HEAD = DK + DV
COLS = 2 * H * HEAD
CHUNKS = 2 * H
WT = 256.0
EPS = 1e-12

P = 128
PACK = 4
T = N // P
HALF = T // 2
HALVES = 2 * B
BANKS = HALF // 2
NARROW = HALF * CHUNKS
WIDE = HALF * H

ROUND_MAGIC = 1.5 * 2.0**23
LOG_MAX = 6.0
SUM_LAG = 2

FLOPS = 2 * B * N * DIM * COLS


def tile_gatedscreeningtile_pa_t_kernel(
    tc, tokens, w_qg, w_kv, sm_log, out_0, out_1, out_2, out_3
):
    nc = tc.nc
    with ExitStack() as ctx:
        ctx.enter_context(tc.manual_schedule())
        const = ctx.enter_context(tc.tile_pool(name="const", bufs=1))
        resident = ctx.enter_context(tc.tile_pool(name="resident", bufs=1))
        stage = ctx.enter_context(tc.tile_pool(name="stage", bufs=3))
        squares = ctx.enter_context(tc.tile_pool(name="squares", bufs=SUM_LAG + 2))
        results = ctx.enter_context(tc.tile_pool(name="results", bufs=4))

        def live(h):
            return 0 <= h < HALVES

        def rows_of(dram, b):
            return dram[b].rearrange("h (p t) d -> p h (t d)", t=T)

        log_window = const.tile([P, H], BF16)
        nc.scalar.dma_start(out=log_window[:], in_=sm_log.partition_broadcast(P))
        w_rows = const.tile([P, 2, DIM], BF16)
        nc.sync.dma_start(out=w_rows[:, 0, :], in_=w_qg)
        nc.sync.dma_start(out=w_rows[:, 1, :], in_=w_kv)
        x_rows = []
        for h in range(HALVES):
            x_h = resident.tile([P, HALF, DIM], BF16, name="x_rows%d" % h)
            first = (h % 2) * HALF
            nc.sync.dma_start(
                out=x_h[:],
                in_=tokens[h // 2].rearrange("(p t) k -> p t k", t=T)[:, first : first + HALF, :],
            )
            x_rows.append(x_h)

        warm = const.tile([P, 1], F32)
        nc.vector.memset(warm[:], 0.0)
        nc.scalar.activation(out=warm[:], in_=warm[:], func=ACT.Silu)

        ident = const.tile([P, P], F32)
        make_identity(nc, ident[:])

        two = const.tile([P, H], F32)
        minus_one = const.tile([P, H], F32)
        position = const.tile([P, T], F32)
        window = const.tile([P, H], F32)
        nc.gpsimd.memset(two[:], 2.0)
        nc.gpsimd.memset(minus_one[:], -1.0)
        nc.gpsimd.iota(
            position[:], pattern=[[1, T]], base=0, channel_multiplier=T,
            allow_small_or_imprecise_dtypes=True,
        )
        nc.gpsimd.tensor_scalar(
            out=window[:], in0=log_window[:], scalar1=LOG_MAX, scalar2=1.0 / math.log(2.0),
            op0=ALU.min, op1=ALU.mult,
        )
        nc.gpsimd.tensor_tensor(out=window[:], in0=two[:], in1=window[:], op=ALU.pow)
        nc.gpsimd.tensor_scalar(
            out=window[:], in0=window[:], scalar1=1.0, scalar2=WT, op0=ALU.add, op1=ALU.min
        )
        cos_window = const.tile([P, H], F32)
        nc.scalar.activation(
            out=cos_window[:], in_=window[:], func=ACT.Sin, scale=-math.pi / WT, bias=math.pi / 2
        )
        per_position = const.tile([P, H], F32)
        nc.gpsimd.tensor_tensor(out=per_position[:], in0=window[:], in1=minus_one[:], op=ALU.pow)
        nc.gpsimd.tensor_scalar_add(out=cos_window[:], in0=cos_window[:], scalar1=1.0)
        nc.gpsimd.tensor_mul(out=per_position[:], in0=per_position[:], in1=cos_window[:])
        turns = const.tile([P, H, T], F32)
        for head in range(H):
            nc.gpsimd.tensor_scalar(
                out=turns[:, head, :], in0=position[:],
                scalar1=per_position[:, head : head + 1], scalar2=0.25,
                op0=ALU.mult, op1=ALU.mult,
            )
        whole = const.tile([P, H, T], F32)
        nc.gpsimd.tensor_scalar(
            out=whole[:], in0=turns[:], scalar1=ROUND_MAGIC, scalar2=ROUND_MAGIC,
            op0=ALU.add, op1=ALU.subtract,
        )
        nc.gpsimd.tensor_sub(out=turns[:], in0=turns[:], in1=whole[:])

        def finish_rotation_table():
            sin_half = const.tile([P, H * T], F32)
            sin_quarter = const.tile([P, H * T], F32)
            flat_turns = turns[:].rearrange("p h t -> p (h t)")
            nc.scalar.activation(out=sin_half[:], in_=flat_turns, func=ACT.Sin, scale=math.pi)
            nc.scalar.activation(
                out=sin_quarter[:], in_=flat_turns, func=ACT.Sin, scale=math.pi / 2
            )
            cos_half = const.tile([P, H * T], F32)
            nc.gpsimd.tensor_mul(out=cos_half[:], in0=sin_quarter[:], in1=sin_quarter[:])
            nc.gpsimd.tensor_scalar(
                out=cos_half[:], in0=cos_half[:], scalar1=-2.0, scalar2=1.0,
                op0=ALU.mult, op1=ALU.add,
            )
            half_sin_x = const.tile([P, H * T], F32)
            nc.gpsimd.tensor_mul(out=half_sin_x[:], in0=sin_half[:], in1=cos_half[:])
            sin_half_squared = const.tile([P, H * T], F32)
            nc.gpsimd.tensor_mul(out=sin_half_squared[:], in0=sin_half[:], in1=sin_half[:])
            table = const.tile([P, 2, H * T, 2, 2], F32, name="rotation")
            for_q_and_k = [P, 2, H * T]
            for diagonal in range(2):
                nc.gpsimd.tensor_scalar(
                    out=table[:, :, :, diagonal, diagonal],
                    in0=sin_half_squared[:].unsqueeze(1).to_broadcast(for_q_and_k),
                    scalar1=-2.0, scalar2=1.0, op0=ALU.mult, op1=ALU.add,
                )
            nc.gpsimd.tensor_scalar_mul(
                out=table[:, :, :, 0, 1],
                in0=half_sin_x[:].unsqueeze(1).to_broadcast(for_q_and_k), scalar1=-2.0,
            )
            nc.gpsimd.tensor_scalar_mul(
                out=table[:, :, :, 1, 0],
                in0=half_sin_x[:].unsqueeze(1).to_broadcast(for_q_and_k), scalar1=2.0,
            )
            return table

        def flip(banks, rows, first):
            words = rows[:].bitcast(F32)
            flipped = banks.tile([P, 2, 2, P], F32, tag="flipped")
            for j in range(2):
                for u in range(2):
                    nc.tensor.transpose(
                        flipped[:, j, u, :], words[:, first + j, u * P : (u + 1) * P], ident[:]
                    )
            return flipped

        def regroup(copy, flipped, grouped):
            copy(
                out=grouped.bitcast(F32).rearrange("p (j r u) -> p j r u", j=2, u=2),
                in_=flipped[:].rearrange("p j u r -> p j r u"),
            )

        BANK_COLS = 2 * P * PACK
        w_codes = const.tile([P, COLS], U32, align_bytes=64)
        w_scales = const.tile([P, COLS], U8, align_bytes=64)
        x_codes = []
        x_scales = []
        for h in range(HALVES):
            x_codes.append(resident.tile([P, HALF * P], U32, name="x_codes%d" % h, align_bytes=64))
            x_scales.append(resident.tile([P, HALF * P], U8, name="x_scales%d" % h, align_bytes=64))

        def project(banks, h):
            products = []
            for i in range(BANKS):
                acc = banks.tile([P, 2, COLS], F32, tag="acc")
                for j in range(2):
                    cols = slice((2 * i + j) * P, (2 * i + j + 1) * P)
                    nc.tensor.matmul_mx(
                        out=acc[:, j, :],
                        lhsT=x_codes[h][:, cols].bitcast(FP8X4),
                        lhsT_scale=x_scales[h][:, cols],
                        rhs=w_codes[:].bitcast(FP8X4),
                        rhs_scale=w_scales[:],
                        start=True,
                        stop=True,
                    )
                products.append(acc[:].rearrange("p j (c d) -> p j c d", d=HEAD))
            return products

        sum_squares = const.tile([P, HALVES, NARROW + WIDE], F32)
        flipped_of = {}
        grouped_of = {}
        acc_of = {}
        squares_of = {}
        gate_of = {}

        with tc.psum_pool(name="flip_banks", bufs=4) as flip_banks, tc.psum_pool(
            name="acc_banks", bufs=4
        ) as acc_banks:
            w_grouped = const.tile([P, BANK_COLS], BF16, align_bytes=64)
            regroup(nc.vector.tensor_copy, flip(flip_banks, w_rows, 0), w_grouped[:])
            nc.vector.quantize_mx(
                out=w_codes[:].bitcast(FP8X4), scales=w_scales[:], in_=w_grouped[:]
            )

            def first_sweep_step(h):
                if live(h + 3):
                    flipped_of[h + 3] = [
                        flip(flip_banks, x_rows[h + 3], 2 * i) for i in range(BANKS)
                    ]
                if live(h + 1):
                    nc.vector.quantize_mx(
                        out=x_codes[h + 1][:].bitcast(FP8X4), scales=x_scales[h + 1][:],
                        in_=grouped_of[h + 1][:],
                    )
                    acc_of[h + 1] = project(acc_banks, h + 1)
                if live(h - SUM_LAG - 1):
                    nc.vector.tensor_scalar_max(
                        out=sum_squares[:, h - SUM_LAG - 1, :],
                        in0=sum_squares[:, h - SUM_LAG - 1, :], scalar1=EPS * EPS,
                    )
                if live(h):
                    if h % 2 == 0:
                        gate_of[h // 2] = results.tile([P, H, T, DV], F32, name="gate", tag="gate")
                    gate = gate_of[h // 2]
                    sq_narrow = squares.tile([P, HALF, CHUNKS, DK], F32, tag="sq_narrow")
                    sq_wide = squares.tile([P, HALF, H, DV], F32, tag="sq_wide")
                    squares_of[h] = (sq_narrow, sq_wide)
                    for i in range(BANKS):
                        acc = acc_of[h][i]
                        here = slice(2 * i, 2 * i + 2)
                        there = slice((h % 2) * HALF + 2 * i, (h % 2) * HALF + 2 * i + 2)
                        nc.scalar.activation(
                            out=sq_narrow[:, here, :, :], in_=acc[:, :, :, 0:DK], func=ACT.Square
                        )
                        nc.scalar.activation(
                            out=sq_wide[:, here, :, :], in_=acc[:, :, H:CHUNKS, DK:HEAD],
                            func=ACT.Square,
                        )
                        nc.scalar.activation(
                            out=gate[:, :, there, :].rearrange("p h j d -> p j h d"),
                            in_=acc[:, :, 0:H, DK:HEAD], func=ACT.Silu,
                        )
                if live(h + 2):
                    grouped = stage.tile([P, BANKS * BANK_COLS], BF16, tag="grouped", align_bytes=64)
                    grouped_of[h + 2] = grouped
                    first_copy = nc.scalar.copy if h % 2 == 0 else nc.vector.tensor_copy
                    regroup(first_copy, flipped_of[h + 2][0], grouped[:, 0:BANK_COLS])
                    regroup(nc.vector.tensor_copy, flipped_of[h + 2][1], grouped[:, BANK_COLS:])
                if live(h - SUM_LAG):
                    sq_narrow, sq_wide = squares_of[h - SUM_LAG]
                    nc.vector.tensor_reduce(
                        out=sum_squares[:, h - SUM_LAG, 0:NARROW],
                        in_=sq_narrow[:].rearrange("p t c d -> p (t c) d"), axis=AXIS.X, op=ALU.add,
                    )
                    nc.vector.tensor_reduce(
                        out=sum_squares[:, h - SUM_LAG, NARROW:],
                        in_=sq_wide[:].rearrange("p t h d -> p (t h) d"), axis=AXIS.X, op=ALU.add,
                    )
                if live(h - 1):
                    gate = gate_of[(h - 1) // 2]
                    there = slice(((h - 1) % 2) * HALF, ((h - 1) % 2 + 1) * HALF)
                    nc.scalar.activation(
                        out=gate[:, :, there, :], in_=gate[:, :, there, :], func=ACT.Tanh
                    )
                    if (h - 1) % 2 == 1:
                        nc.sync.dma_start(
                            out=rows_of(out_1, (h - 1) // 2),
                            in_=gate[:].rearrange("p h t d -> p h (t d)"),
                        )

            for h in range(-3, HALVES // 2):
                first_sweep_step(h)
            rotation = finish_rotation_table()
            for h in range(HALVES // 2, HALVES + SUM_LAG + 2):
                first_sweep_step(h)

        inverse_norm = const.tile([P, HALVES, NARROW + WIDE], F32)
        for part in (slice(0, HALVES // 2), slice(HALVES // 2, HALVES)):
            nc.scalar.activation(
                out=inverse_norm[:, part, :], in_=sum_squares[:, part, :],
                func=ACT.Abs_reciprocal_sqrt,
            )

        again_banks = ctx.enter_context(tc.psum_pool(name="again_banks", bufs=8))
        AHEAD = 2
        for h in range(AHEAD):
            acc_of[h] = project(again_banks, h)
        for h in range(HALVES):
            b = h // 2
            if live(h + AHEAD):
                acc_of[h + AHEAD] = project(again_banks, h + AHEAD)
            if h % 2 == 0:
                qk = results.tile([P, CHUNKS, T, DK], F32, tag="qk")
                v_n = results.tile([P, H, T, DV], F32, tag="v_n")
            for i in range(BANKS):
                there = slice((h % 2) * HALF + 2 * i, (h % 2) * HALF + 2 * i + 2)
                narrow = inverse_norm[:, h, 2 * i * CHUNKS : (2 * i + 2) * CHUNKS]
                nc.vector.tensor_tensor(
                    out=qk[:, :, there, :].rearrange("p c j d -> p j c d"),
                    in0=acc_of[h][i][:, :, :, 0:DK],
                    in1=narrow.rearrange("p (j c) -> p j c", j=2)
                    .unsqueeze(3)
                    .to_broadcast([P, 2, CHUNKS, DK]),
                    op=ALU.mult,
                )
            if h % 2 == 1:
                pair = qk[:].rearrange("p c t d -> p (c t) d")[:, :, 0:2]
                products = stage.tile([P, CHUNKS * T, 2, 2], F32, tag="products")
                nc.gpsimd.tensor_tensor(
                    out=products[:],
                    in0=pair.unsqueeze(2).to_broadcast([P, CHUNKS * T, 2, 2]),
                    in1=rotation[:].rearrange("p w g r c -> p (w g) r c"),
                    op=ALU.mult,
                )
                nc.gpsimd.tensor_add(
                    out=pair, in0=products[:, :, :, 0], in1=products[:, :, :, 1]
                )
            for i in range(BANKS):
                there = slice((h % 2) * HALF + 2 * i, (h % 2) * HALF + 2 * i + 2)
                wide = inverse_norm[:, h, NARROW + 2 * i * H : NARROW + (2 * i + 2) * H]
                nc.vector.tensor_tensor(
                    out=v_n[:, :, there, :].rearrange("p h j d -> p j h d"),
                    in0=acc_of[h][i][:, :, H:CHUNKS, DK:HEAD],
                    in1=wide.rearrange("p (j h) -> p j h", j=2)
                    .unsqueeze(3)
                    .to_broadcast([P, 2, H, DV]),
                    op=ALU.mult,
                )
            if h % 2 == 1:
                nc.sync.dma_start(
                    out=rows_of(out_3, b), in_=v_n[:].rearrange("p h t d -> p h (t d)")
                )
                nc.sync.dma_start(
                    out=rows_of(out_0, b),
                    in_=qk[:, 0:H, :, :].rearrange("p h t d -> p h (t d)"),
                )
                nc.sync.dma_start(
                    out=rows_of(out_2, b),
                    in_=qk[:, H:CHUNKS, :, :].rearrange("p h t d -> p h (t d)"),
                )
